import numpy as np
import ml_dtypes


def mxq(x, axis, fmt="e4m3"):
    dtype, down = {"e4m3": (ml_dtypes.float8_e4m3fn, 7), "e5m2": (ml_dtypes.float8_e5m2, 14)}[fmt]
    v = np.moveaxis(np.asarray(x, np.float32).astype(ml_dtypes.bfloat16).astype(np.float64), axis, -1)
    blocks = v.reshape(v.shape[:-1] + (-1, 32))
    amax = np.abs(blocks).max(-1, keepdims=True)
    byte = np.maximum(np.where(amax > 0, np.frexp(amax)[1] - 1 + 127, 0) - down, 1)
    scale = np.exp2(byte - 127.0)
    codes = (blocks / scale).astype(np.float32).astype(dtype).astype(np.float64)
    return np.moveaxis((codes * scale).reshape(v.shape), -1, axis)


WIDE = False


def mx_kscale(k):
    if not WIDE:
        return np.ones(k)
    levels = np.array([10, -10, 5, -5, 0])
    if k % 512:
        return np.exp2(np.random.permutation(np.resize(levels, k // 32))).repeat(32)
    a = np.empty((k // 512, 16))
    for p in range(k // 512):
        a[p, :8] = np.random.permutation(np.resize(levels, 8))
        for g in range(8):
            far = levels[np.abs(levels - a[p, g]) >= 10]
            a[p, g + 8] = far[np.random.randint(len(far))]
    return np.exp2(a.ravel()).repeat(32)


BF16 = ml_dtypes.bfloat16


def bf(x):
    return np.asarray(x, np.float32).astype(BF16)


def f64(x):
    return np.asarray(x).astype(np.float64)


B, A, G, H1, H2 = 1024, 128, 5, 2048, 2048
SLOPE = 0.4


def leaky(v):
    return np.where(v >= 0.0, v, SLOPE * v)


def setup_inputs():
    s, t = mx_kscale(H1), mx_kscale(H2)
    keep = np.where(np.random.uniform(size=(B, A)) > 0.2, 1.0, 0.0)
    return {"x": bf(np.random.standard_normal((B, A * G)) * np.repeat(keep, G, axis=1)),
            "h1": bf(leaky(np.random.standard_normal((B, H1))) * s),
            "W2": bf(np.random.standard_normal((H1, H2)) * 1.3 / np.sqrt(H1) / s[:, None] * t),
            "b2": bf(np.random.standard_normal(H2) * 0.3 * t),
            "W3": bf(np.random.standard_normal((H2, A)) * 2.5 / np.sqrt(H2) / t[:, None]),
            "b3": bf(np.random.standard_normal(A) * 0.5)}


def reference(x, h1, W2, b2, W3, b3):
    gsum = f64(x).reshape(B, A, G).sum(axis=-1)
    mask = gsum != 0.0
    h2 = leaky((mxq(f64(h1), 1, "e4m3") @ mxq(f64(W2), 0, "e4m3")) + f64(b2))
    logits = (mxq(h2, 1, "e4m3") @ mxq(f64(W3), 0, "e4m3")) + f64(b3)
    logits = np.where(mask, logits, -np.inf)
    e = np.exp(logits - logits.max(axis=1, keepdims=True))
    return e / e.sum(axis=1, keepdims=True)

@@ -1,0 +1,249 @@
+from contextlib import ExitStack
+
+import concourse.mybir as mybir
+from concourse.masks import make_identity
+
+F32 = mybir.dt.float32
+BF16 = mybir.dt.bfloat16
+U32 = mybir.dt.uint32
+U8 = mybir.dt.uint8
+FP8X4 = mybir.dt.float8_e4m3fn_x4
+ALU = mybir.AluOpType
+ACT = mybir.ActivationFunctionType
+AX = mybir.AxisListType
+
+P = 128
+B, A, G, H1, H2 = 1024, 128, 5, 2048, 2048
+SLOPE = 0.4
+BIG = 1.0e30
+FLOPS = 2 * B * H1 * H2 + 2 * B * H2 * A
+
+WVS = (288, 176, 176, 112)
+LAG = 1
+UNITS = [(0, 0, 4), (0, 4, 4), (1, 0, 4), (1, 4, 4), (2, 0, 4), (2, 4, 4), (3, 0, 2), (3, 2, 2), (3, 4, 2), (3, 6, 2)]
+HEAD = 2
+
+
+def tile_dqn_pa_kernel(tc, x, h1, W2, b2, W3, b3, out):
+    nc = tc.nc
+    with ExitStack() as ctx:
+        const = ctx.enter_context(tc.tile_pool(name="const", bufs=1))
+        raw = ctx.enter_context(tc.tile_pool(name="raw", bufs=12))
+        big = ctx.enter_context(tc.tile_pool(name="big", bufs=5))
+        w2gp = ctx.enter_context(tc.tile_pool(name="w2gp", bufs=4))
+        h2gp = ctx.enter_context(tc.tile_pool(name="h2gp", bufs=2))
+        sm = ctx.enter_context(tc.tile_pool(name="sm", bufs=2))
+        psum = ctx.enter_context(tc.psum_pool(name="psum", bufs=8))
+
+        ident = const.tile([P, P], F32, name="ident")
+        make_identity(nc, ident[:])
+        warm = const.tile([P, 2], F32, name="warm")
+        nc.vector.memset(warm[:], 0.0)
+        nc.scalar.activation(out=warm[:, 1:2], in_=warm[:, 0:1], func=ACT.Exp)
+        b2T = const.tile([P, 4, 4], BF16, name="b2T")
+        nc.scalar.dma_start(out=b2T[:], in_=b2.rearrange("(g p t) -> p g t", p=P, t=4))
+        b3row = const.tile([P, A], BF16, name="b3row")
+        nc.vector.memset(b3row[:], 0.0)
+        ones = const.tile([P, P], BF16, name="ones")
+        nc.vector.memset(ones[:], 1.0)
+
+        h1codes = const.tile([P, 4, B], U32, name="h1codes", align_bytes=64)
+        h1sc = const.tile([P, 4, B], U8, name="h1sc", align_bytes=64)
+        w2codes = const.tile([P, 4, H2], U32, name="w2codes", align_bytes=64)
+        w2sc = const.tile([P, 4, H2], U8, name="w2sc", align_bytes=64)
+        h2codes = const.tile([P, 4, B], U32, name="h2codes", align_bytes=64)
+        h2sc = const.tile([P, 4, B], U8, name="h2sc", align_bytes=64)
+        w3codes = const.tile([P, 4 * A], U32, name="w3codes", align_bytes=64)
+        w3sc = const.tile([P, 4 * A], U8, name="w3sc", align_bytes=64)
+
+        xparts = []
+        h1raw = []
+
+        def load_x(i0, n):
+            t = raw.tile([P, n, A * G], BF16, name="xraw%d" % i0, tag="raw")
+            nc.sync.dma_start(out=t[:], in_=x[i0 * P:(i0 + n) * P, :].rearrange("(i p) c -> p i c", p=P))
+            xparts.append((i0, n, t))
+
+        def load_h1(i):
+            t = raw.tile([P, H1], BF16, name="h1raw%d" % i, tag="raw")
+            nc.sync.dma_start(out=t[:], in_=h1[i * P:(i + 1) * P, :])
+            h1raw.append(t)
+
+        load_h1(0)
+        load_x(0, 3)
+        load_h1(1)
+        load_h1(2)
+        load_x(3, 3)
+        load_h1(3)
+        load_h1(4)
+        load_x(6, 2)
+        for i in range(5, 8):
+            load_h1(i)
+        nc.sync.dma_start(out=b3row[0:1, :], in_=b3.rearrange("(o a) -> o a", o=1))
+        w2raw = []
+        for k in range(16):
+            g, c = k // 4, k % 4
+            t = raw.tile([P, 4, 512], BF16, name="w2raw%d" % k, tag="raw")
+            nc.sync.dma_start(
+                out=t[:],
+                in_=W2[512 * c:512 * c + 512, 512 * g:512 * g + 512].rearrange("(p t) w -> p t w", t=4),
+            )
+            w2raw.append(t)
+        w3raw = raw.tile([P, 4, 4 * A], BF16, name="w3raw", tag="raw")
+        nc.sync.dma_start(out=w3raw[:], in_=W3.rearrange("(g p t) a -> p g (t a)", p=P, t=4))
+
+        def h1_half(bh):
+            units = [
+                big.tile([P, 2 * 512 * 4], BF16, name="h1g%d_%d" % (bh, gp), tag="big", align_bytes=64)
+                for gp in range(2)
+            ]
+            for ii in range(4):
+                words = h1raw[4 * bh + ii][:].bitcast(F32)
+                for gp in range(2):
+                    bank = psum.tile([P, 2, 2, P], F32, name="trb%d_%d_%d" % (bh, ii, gp), tag="bank")
+                    for gg in range(2):
+                        for u in range(2):
+                            w0 = 256 * (2 * gp + gg)
+                            nc.tensor.transpose(bank[:, gg, u, :], words[:, w0 + u:w0 + 256:2], ident[:])
+                    dst = units[gp][:].bitcast(F32).rearrange("p (g b u) -> p g b u", g=2, u=2)
+                    dst = dst[:, :, ii * P:(ii + 1) * P, :]
+                    nc.scalar.copy(out=dst, in_=bank[:].rearrange("p g u b -> p g b u"))
+            for c in range(4):
+                nc.vector.quantize_mx(
+                    out=h1codes[:, c, 512 * bh:512 * bh + 512].bitcast(FP8X4),
+                    scales=h1sc[:, c, 512 * bh:512 * bh + 512],
+                    in_=units[c // 2][:, 2048 * (c % 2):2048 * (c % 2) + 2048],
+                )
+
+        def w2_chunk(k):
+            g, c = k // 4, k % 4
+            jv = WVS[g] // 4
+            src = w2raw[k]
+            grp = w2gp.tile([P, 512, 4], BF16, name="w2g%d" % k, tag="w2g", align_bytes=64)
+            dst = grp[:].rearrange("p (i j) t -> p j t i", i=4)
+            src = src[:].rearrange("p t (j i) -> p j t i", i=4)
+            nc.vector.tensor_copy(out=dst[:, 0:jv], in_=src[:, 0:jv])
+            nc.scalar.copy(out=dst[:, jv:P], in_=src[:, jv:P])
+            nc.vector.quantize_mx(
+                out=w2codes[:, c, 512 * g:512 * g + 512].bitcast(FP8X4),
+                scales=w2sc[:, c, 512 * g:512 * g + 512],
+                in_=grp[:].rearrange("p w t -> p (w t)"),
+            )
+
+        def mm1(u, c_outer):
+            g, i0, nb = UNITS[u]
+            n = P * nb
+            per = 512 // n
+            banks = [psum.tile([P, per, n], F32, name="mm%d_%d" % (u, j), tag="bank") for j in range(4 // per)]
+            groups = [banks[t // per][:, t % per, :] for t in range(4)]
+            if c_outer:
+                order = [(c, t) for c in range(4) for t in range(4)]
+            else:
+                order = [(c, t) for t in range(4) for c in range(4)]
+            for (c, t) in order:
+                m = 4 * g + t
+                nc.tensor.matmul_mx(
+                    out=groups[t],
+                    lhsT=w2codes[:, c, m * P:(m + 1) * P].bitcast(FP8X4),
+                    lhsT_scale=w2sc[:, c, m * P:(m + 1) * P],
+                    rhs=h1codes[:, c, P * i0:P * i0 + n].bitcast(FP8X4),
+                    rhs_scale=h1sc[:, c, P * i0:P * i0 + n],
+                    start=(c == 0),
+                    stop=(c == 3),
+                )
+            return groups
+
+        def epilogue(u, groups):
+            g, i0, nb = UNITS[u]
+            n = P * nb
+            a = big.tile([P, 4, n], F32, name="a%d" % u, tag="big", align_bytes=64)
+            for t in range(4):
+                nc.scalar.activation(out=a[:, t, :], in_=groups[t], func=ACT.Identity,
+                                     bias=b2T[:, g, t:t + 1], scale=1.0)
+            h2g = h2gp.tile([P, n, 4], BF16, name="h2g%d" % u, tag="h2g", align_bytes=64)
+            av = a[:].rearrange("p t b -> p b t")
+            nc.vector.scalar_tensor_tensor(out=h2g[:], in0=av, scalar=SLOPE, in1=av,
+                                           op0=ALU.mult, op1=ALU.max)
+            nc.vector.quantize_mx(
+                out=h2codes[:, g, P * i0:P * i0 + n].bitcast(FP8X4),
+                scales=h2sc[:, g, P * i0:P * i0 + n],
+                in_=h2g[:].rearrange("p b t -> p (b t)"),
+            )
+
+        def head(j):
+            lg = psum.tile([P, HEAD, A], F32, name="lg%d" % j, tag="bank")
+            for ii in range(HEAD):
+                i = HEAD * j + ii
+                for g in range(4):
+                    nc.tensor.matmul_mx(
+                        out=lg[:, ii, :],
+                        lhsT=h2codes[:, g, i * P:(i + 1) * P].bitcast(FP8X4),
+                        lhsT_scale=h2sc[:, g, i * P:(i + 1) * P],
+                        rhs=w3codes[:, g * A:(g + 1) * A].bitcast(FP8X4),
+                        rhs_scale=w3sc[:, g * A:(g + 1) * A],
+                        start=(g == 0),
+                        stop=(g == 3),
+                    )
+            nlp = sm.tile([P, HEAD, A], F32, name="nlp%d" % j, tag="nlp")
+            nc.vector.tensor_tensor(out=nlp[:], in0=nbm[:, HEAD * j:HEAD * (j + 1), :], in1=lg[:], op=ALU.subtract)
+            nmx = sm.tile([P, HEAD], F32, name="nmx%d" % j, tag="nmx")
+            nc.vector.tensor_reduce(out=nmx[:], in_=nlp[:], axis=AX.X, op=ALU.min)
+            e = sm.tile([P, HEAD, A], F32, name="e%d" % j, tag="e")
+            s = sm.tile([P, HEAD], F32, name="s%d" % j, tag="s")
+            for ii in range(HEAD):
+                nc.scalar.activation(out=e[:, ii, :], in_=nlp[:, ii, :], func=ACT.Exp,
+                                     bias=nmx[:, ii:ii + 1], scale=-1.0, accum_out=s[:, ii:ii + 1])
+            r = sm.tile([P, HEAD], F32, name="r%d" % j, tag="r")
+            nc.vector.reciprocal(out=r[:], in_=s[:])
+            for ii in range(HEAD):
+                nc.scalar.activation(out=e[:, ii, :], in_=e[:, ii, :], func=ACT.Copy, scale=r[:, ii:ii + 1])
+            rows = P * HEAD
+            nc.sync.dma_start(out=out[rows * j:rows * (j + 1), :].rearrange("(i p) a -> p i a", p=P), in_=e[:])
+
+        nbm = const.tile([P, 8, A], F32, name="nbm")
+        for (i0, n, t) in xparts:
+            for i in range(n):
+                nc.vector.tensor_reduce(out=nbm[:, i0 + i, :],
+                                        in_=t[:, i, :].rearrange("p (a j) -> p a j", j=G),
+                                        axis=AX.X, op=ALU.add)
+        nc.vector.tensor_scalar(out=nbm[:], in0=nbm[:], scalar1=0.0, scalar2=BIG,
+                                op0=ALU.is_equal, op1=ALU.mult)
+
+        h1_half(0)
+        h1_half(1)
+
+        b3ps = psum.tile([P, 512], F32, name="b3ps", tag="bank")
+        nc.tensor.matmul(out=b3ps[:, 0:A], lhsT=ones[:], rhs=b3row[:], start=True, stop=True)
+        nc.vector.tensor_tensor(out=nbm[:], in0=nbm[:],
+                                in1=b3ps[:, 0:A].unsqueeze(1).to_broadcast([P, 8, A]), op=ALU.subtract)
+
+        for k in range(4):
+            w2_chunk(k)
+        nxt = 4
+        waiting = []
+        heads = 0
+        covered = 0
+        for u in range(len(UNITS)):
+            waiting.append((u, mm1(u, u == 0)))
+            for z in range(2):
+                if nxt < 16:
+                    w2_chunk(nxt)
+                    nxt += 1
+            if len(waiting) > LAG:
+                (v, groups) = waiting.pop(0)
+                epilogue(v, groups)
+                if UNITS[v][0] == 3:
+                    covered += UNITS[v][2]
+            if u == 5:
+                w3g = const.tile([P, 4, A, 4], BF16, name="w3g", align_bytes=64)
+                nc.scalar.copy(out=w3g[:], in_=w3raw[:].rearrange("p g (t a) -> p g a t", t=4))
+                nc.vector.quantize_mx(out=w3codes[:].bitcast(FP8X4), scales=w3sc[:],
+                                      in_=w3g[:].rearrange("p g a t -> p (g a t)"))
+            if True and covered >= HEAD * (heads + 2):
+                head(heads)
+                heads += 1
+        for (v, groups) in waiting:
+            epilogue(v, groups)
+        while heads * HEAD < 8:
+            head(heads)
+            heads += 1

@@ -15,7 +15,7 @@ AX = mybir.AxisListType
 P = 128
 B, A, G, H1, H2 = 1024, 128, 5, 2048, 2048
 SLOPE = 0.4
-BIG = 1.0e30
+BIG = 2.0 ** 100
 FLOPS = 2 * B * H1 * H2 + 2 * B * H2 * A
 
 WVS = (288, 176, 176, 112)
@@ -44,8 +44,8 @@ def tile_dqn_pa_kernel(tc, x, h1, W2, b2, W3, b3, out):
         nc.scalar.dma_start(out=b2T[:], in_=b2.rearrange("(g p t) -> p g t", p=P, t=4))
         b3row = const.tile([P, A], BF16, name="b3row")
         nc.vector.memset(b3row[:], 0.0)
-        ones = const.tile([P, P], BF16, name="ones")
-        nc.vector.memset(ones[:], 1.0)
+        tiny = const.tile([P, P], BF16, name="tiny")
+        nc.vector.memset(tiny[:], 1.0 / BIG)
 
         h1codes = const.tile([P, 4, B], U32, name="h1codes", align_bytes=64)
         h1sc = const.tile([P, 4, B], U8, name="h1sc", align_bytes=64)
@@ -115,15 +115,21 @@ def tile_dqn_pa_kernel(tc, x, h1, W2, b2, W3, b3, out):
                     in_=units[c // 2][:, 2048 * (c % 2):2048 * (c % 2) + 2048],
                 )
 
-        def w2_chunk(k):
-            g, c = k // 4, k % 4
-            jv = WVS[g] // 4
+        w2grp = {}
+
+        def w2_regroup(k):
+            jv = WVS[k // 4] // 4
             src = w2raw[k]
             grp = w2gp.tile([P, 512, 4], BF16, name="w2g%d" % k, tag="w2g", align_bytes=64)
             dst = grp[:].rearrange("p (i j) t -> p j t i", i=4)
             src = src[:].rearrange("p t (j i) -> p j t i", i=4)
             nc.vector.tensor_copy(out=dst[:, 0:jv], in_=src[:, 0:jv])
             nc.scalar.copy(out=dst[:, jv:P], in_=src[:, jv:P])
+            w2grp[k] = grp
+
+        def w2_quantise(k):
+            g, c = k // 4, k % 4
+            grp = w2grp[k]
             nc.vector.quantize_mx(
                 out=w2codes[:, c, 512 * g:512 * g + 512].bitcast(FP8X4),
                 scales=w2sc[:, c, 512 * g:512 * g + 512],
@@ -164,6 +170,11 @@ def tile_dqn_pa_kernel(tc, x, h1, W2, b2, W3, b3, out):
             av = a[:].rearrange("p t b -> p b t")
             nc.vector.scalar_tensor_tensor(out=h2g[:], in0=av, scalar=SLOPE, in1=av,
                                            op0=ALU.mult, op1=ALU.max)
+            return h2g
+
+        def h2_quantise(u, h2g):
+            g, i0, nb = UNITS[u]
+            n = P * nb
             nc.vector.quantize_mx(
                 out=h2codes[:, g, P * i0:P * i0 + n].bitcast(FP8X4),
                 scales=h2sc[:, g, P * i0:P * i0 + n],
@@ -185,7 +196,8 @@ def tile_dqn_pa_kernel(tc, x, h1, W2, b2, W3, b3, out):
                         stop=(g == 3),
                     )
             nlp = sm.tile([P, HEAD, A], F32, name="nlp%d" % j, tag="nlp")
-            nc.vector.tensor_tensor(out=nlp[:], in0=nbm[:, HEAD * j:HEAD * (j + 1), :], in1=lg[:], op=ALU.subtract)
+            nc.vector.scalar_tensor_tensor(out=nlp[:], in0=nbm[:, HEAD * j:HEAD * (j + 1), :], scalar=BIG,
+                                           in1=lg[:], op0=ALU.mult, op1=ALU.subtract)
             nmx = sm.tile([P, HEAD], F32, name="nmx%d" % j, tag="nmx")
             nc.vector.tensor_reduce(out=nmx[:], in_=nlp[:], axis=AX.X, op=ALU.min)
             e = sm.tile([P, HEAD, A], F32, name="e%d" % j, tag="e")
@@ -206,44 +218,50 @@ def tile_dqn_pa_kernel(tc, x, h1, W2, b2, W3, b3, out):
                 nc.vector.tensor_reduce(out=nbm[:, i0 + i, :],
                                         in_=t[:, i, :].rearrange("p (a j) -> p a j", j=G),
                                         axis=AX.X, op=ALU.add)
-        nc.vector.tensor_scalar(out=nbm[:], in0=nbm[:], scalar1=0.0, scalar2=BIG,
-                                op0=ALU.is_equal, op1=ALU.mult)
 
         h1_half(0)
         h1_half(1)
 
         b3ps = psum.tile([P, 512], F32, name="b3ps", tag="bank")
-        nc.tensor.matmul(out=b3ps[:, 0:A], lhsT=ones[:], rhs=b3row[:], start=True, stop=True)
-        nc.vector.tensor_tensor(out=nbm[:], in0=nbm[:],
-                                in1=b3ps[:, 0:A].unsqueeze(1).to_broadcast([P, 8, A]), op=ALU.subtract)
+        nc.tensor.matmul(out=b3ps[:, 0:A], lhsT=tiny[:], rhs=b3row[:], start=True, stop=True)
+        nc.vector.scalar_tensor_tensor(out=nbm[:], in0=nbm[:], scalar=0.0,
+                                       in1=b3ps[:, 0:A].unsqueeze(1).to_broadcast([P, 8, A]),
+                                       op0=ALU.is_equal, op1=ALU.subtract)
 
         for k in range(4):
-            w2_chunk(k)
+            w2_regroup(k)
+        for k in range(4):
+            w2_quantise(k)
         nxt = 4
         waiting = []
         heads = 0
         covered = 0
         for u in range(len(UNITS)):
             waiting.append((u, mm1(u, u == 0)))
-            for z in range(2):
-                if nxt < 16:
-                    w2_chunk(nxt)
-                    nxt += 1
+            ks = range(nxt, min(nxt + 2, 16))
+            nxt += 2
+            for k in ks:
+                w2_regroup(k)
+            done = None
             if len(waiting) > LAG:
                 (v, groups) = waiting.pop(0)
-                epilogue(v, groups)
-                if UNITS[v][0] == 3:
-                    covered += UNITS[v][2]
+                done = (v, epilogue(v, groups))
+            for k in ks:
+                w2_quantise(k)
             if u == 5:
                 w3g = const.tile([P, 4, A, 4], BF16, name="w3g", align_bytes=64)
                 nc.scalar.copy(out=w3g[:], in_=w3raw[:].rearrange("p g (t a) -> p g a t", t=4))
                 nc.vector.quantize_mx(out=w3codes[:].bitcast(FP8X4), scales=w3sc[:],
                                       in_=w3g[:].rearrange("p g a t -> p (g a t)"))
-            if True and covered >= HEAD * (heads + 2):
+            if done:
+                h2_quantise(done[0], done[1])
+                if UNITS[done[0]][0] == 3:
+                    covered += UNITS[done[0]][2]
+            if covered >= HEAD * (heads + 2):
                 head(heads)
                 heads += 1
         for (v, groups) in waiting:
-            epilogue(v, groups)
+            h2_quantise(v, epilogue(v, groups))
         while heads * HEAD < 8:
             head(heads)
             heads += 1

@@ -18,7 +18,8 @@ SLOPE = 0.4
 BIG = 2.0 ** 100
 FLOPS = 2 * B * H1 * H2 + 2 * B * H2 * A
 
-WVS = (288, 176, 176, 112)
+WVS = (256, 192, 192, 128)
+RUN = 8
 LAG = 1
 UNITS = [(0, 0, 4), (0, 4, 4), (1, 0, 4), (1, 4, 4), (2, 0, 4), (2, 4, 4), (3, 0, 2), (3, 2, 2), (3, 4, 2), (3, 6, 2)]
 HEAD = 2
@@ -40,8 +41,11 @@ def tile_dqn_pa_kernel(tc, x, h1, W2, b2, W3, b3, out):
         warm = const.tile([P, 2], F32, name="warm")
         nc.vector.memset(warm[:], 0.0)
         nc.scalar.activation(out=warm[:, 1:2], in_=warm[:, 0:1], func=ACT.Exp)
-        b2T = const.tile([P, 4, 4], BF16, name="b2T")
-        nc.scalar.dma_start(out=b2T[:], in_=b2.rearrange("(g p t) -> p g t", p=P, t=4))
+        b2rows = const.tile([P, P], BF16, name="b2rows")
+        nc.vector.memset(b2rows[:], 0.0)
+        b2v = b2.rearrange("(g q b i) -> g b q i", g=4, b=4, i=RUN)
+        for g in range(4):
+            nc.scalar.dma_start(out=b2rows[4 * g:4 * g + 4, :].rearrange("b (q i) -> b q i", i=RUN), in_=b2v[g])
         b3row = const.tile([P, A], BF16, name="b3row")
         nc.vector.memset(b3row[:], 0.0)
         tiny = const.tile([P, P], BF16, name="tiny")
@@ -89,8 +93,11 @@ def tile_dqn_pa_kernel(tc, x, h1, W2, b2, W3, b3, out):
                 in_=W2[512 * c:512 * c + 512, 512 * g:512 * g + 512].rearrange("(p t) w -> p t w", t=4),
             )
             w2raw.append(t)
-        w3raw = raw.tile([P, 4, 4 * A], BF16, name="w3raw", tag="raw")
-        nc.sync.dma_start(out=w3raw[:], in_=W3.rearrange("(g p t) a -> p g (t a)", p=P, t=4))
+        w3raw = raw.tile([P, 4, 4, A], BF16, name="w3raw", tag="raw")
+        w3v = W3.rearrange("(g q b i) a -> g i q b a", g=4, b=4, i=RUN)
+        for g in range(4):
+            for i in range(RUN):
+                nc.sync.dma_start(out=w3raw[i:P:RUN, g, :, :], in_=w3v[g, i])
 
         def h1_half(bh):
             units = [
@@ -118,13 +125,13 @@ def tile_dqn_pa_kernel(tc, x, h1, W2, b2, W3, b3, out):
         w2grp = {}
 
         def w2_regroup(k):
-            jv = WVS[k // 4] // 4
+            qv = WVS[k // 4] // (4 * RUN)
             src = w2raw[k]
             grp = w2gp.tile([P, 512, 4], BF16, name="w2g%d" % k, tag="w2g", align_bytes=64)
-            dst = grp[:].rearrange("p (i j) t -> p j t i", i=4)
-            src = src[:].rearrange("p t (j i) -> p j t i", i=4)
-            nc.vector.tensor_copy(out=dst[:, 0:jv], in_=src[:, 0:jv])
-            nc.scalar.copy(out=dst[:, jv:P], in_=src[:, jv:P])
+            dst = grp[:].rearrange("p (b q i) t -> p q b t i", b=4, i=RUN)
+            src = src[:].rearrange("p t (q b i) -> p q b t i", b=4, i=RUN)
+            nc.vector.tensor_copy(out=dst[:, 0:qv], in_=src[:, 0:qv])
+            nc.scalar.copy(out=dst[:, qv:], in_=src[:, qv:])
             w2grp[k] = grp
 
         def w2_quantise(k):
@@ -165,7 +172,7 @@ def tile_dqn_pa_kernel(tc, x, h1, W2, b2, W3, b3, out):
             a = big.tile([P, 4, n], F32, name="a%d" % u, tag="big", align_bytes=64)
             for t in range(4):
                 nc.scalar.activation(out=a[:, t, :], in_=groups[t], func=ACT.Identity,
-                                     bias=b2T[:, g, t:t + 1], scale=1.0)
+                                     bias=b2T[:, 4 * g + t:4 * g + t + 1], scale=1.0)
             h2g = h2gp.tile([P, n, 4], BF16, name="h2g%d" % u, tag="h2g", align_bytes=64)
             av = a[:].rearrange("p t b -> p b t")
             nc.vector.scalar_tensor_tensor(out=h2g[:], in0=av, scalar=SLOPE, in1=av,
@@ -222,6 +229,13 @@ def tile_dqn_pa_kernel(tc, x, h1, W2, b2, W3, b3, out):
         h1_half(0)
         h1_half(1)
 
+        b2rows32 = const.tile([P, P], F32, name="b2rows32")
+        nc.vector.tensor_copy(out=b2rows32[:], in_=b2rows[:])
+        b2ps = psum.tile([P, 512], F32, name="b2ps", tag="bank")
+        nc.tensor.transpose(b2ps[:, 0:P], b2rows32[:], ident[:])
+        b2T = const.tile([P, 16], F32, name="b2T")
+        nc.vector.tensor_copy(out=b2T[:], in_=b2ps[:, 0:16])
+
         b3ps = psum.tile([P, 512], F32, name="b3ps", tag="bank")
         nc.tensor.matmul(out=b3ps[:, 0:A], lhsT=tiny[:], rhs=b3row[:], start=True, stop=True)
         nc.vector.scalar_tensor_tensor(out=nbm[:], in0=nbm[:], scalar=0.0,
@@ -250,7 +264,7 @@ def tile_dqn_pa_kernel(tc, x, h1, W2, b2, W3, b3, out):
                 w2_quantise(k)
             if u == 5:
                 w3g = const.tile([P, 4, A, 4], BF16, name="w3g", align_bytes=64)
-                nc.scalar.copy(out=w3g[:], in_=w3raw[:].rearrange("p g (t a) -> p g a t", t=4))
+                nc.scalar.copy(out=w3g[:], in_=w3raw[:].rearrange("p g t a -> p g a t"))
                 nc.vector.quantize_mx(out=w3codes[:].bitcast(FP8X4), scales=w3sc[:],
                                       in_=w3g[:].rearrange("p g a t -> p (g a t)"))
             if done:

@@ -21,7 +21,7 @@ FLOPS = 2 * B * H1 * H2 + 2 * B * H2 * A
 WVS = (256, 192, 192, 128)
 RUN = 8
 LAG = 1
-UNITS = [(0, 0, 4), (0, 4, 4), (1, 0, 4), (1, 4, 4), (2, 0, 4), (2, 4, 4), (3, 0, 2), (3, 2, 2), (3, 4, 2), (3, 6, 2)]
+UNITS = [(g, i0, 4) for g in range(4) for i0 in (0, 4)]
 HEAD = 2
 
 
@@ -33,7 +33,7 @@ def tile_dqn_pa_kernel(tc, x, h1, W2, b2, W3, b3, out):
         big = ctx.enter_context(tc.tile_pool(name="big", bufs=5))
         w2gp = ctx.enter_context(tc.tile_pool(name="w2gp", bufs=4))
         h2gp = ctx.enter_context(tc.tile_pool(name="h2gp", bufs=2))
-        sm = ctx.enter_context(tc.tile_pool(name="sm", bufs=2))
+        sm = ctx.enter_context(tc.tile_pool(name="sm", bufs=4))
         psum = ctx.enter_context(tc.psum_pool(name="psum", bufs=8))
 
         ident = const.tile([P, P], F32, name="ident")
@@ -64,8 +64,10 @@ def tile_dqn_pa_kernel(tc, x, h1, W2, b2, W3, b3, out):
         h1raw = []
 
         def load_x(i0, n):
+            r0 = i0 // 4 * 4 * P
             t = raw.tile([P, n, A * G], BF16, name="xraw%d" % i0, tag="raw")
-            nc.sync.dma_start(out=t[:], in_=x[i0 * P:(i0 + n) * P, :].rearrange("(i p) c -> p i c", p=P))
+            rows = x[r0:r0 + 4 * P, :].rearrange("(p i) c -> p i c", i=4)
+            nc.sync.dma_start(out=t[:], in_=rows[:, i0 % 4:i0 % 4 + n, :])
             xparts.append((i0, n, t))
 
         def load_h1(i):
@@ -74,10 +76,11 @@ def tile_dqn_pa_kernel(tc, x, h1, W2, b2, W3, b3, out):
             h1raw.append(t)
 
         load_h1(0)
-        load_x(0, 3)
+        load_x(0, 2)
         load_h1(1)
+        load_x(2, 2)
         load_h1(2)
-        load_x(3, 3)
+        load_x(4, 2)
         load_h1(3)
         load_h1(4)
         load_x(6, 2)
@@ -99,11 +102,14 @@ def tile_dqn_pa_kernel(tc, x, h1, W2, b2, W3, b3, out):
             for i in range(RUN):
                 nc.sync.dma_start(out=w3raw[i:P:RUN, g, :, :], in_=w3v[g, i])
 
+        h1g = {}
+
         def h1_half(bh):
             units = [
                 big.tile([P, 2 * 512 * 4], BF16, name="h1g%d_%d" % (bh, gp), tag="big", align_bytes=64)
                 for gp in range(2)
             ]
+            h1g[bh] = units
             for ii in range(4):
                 words = h1raw[4 * bh + ii][:].bitcast(F32)
                 for gp in range(2):
@@ -115,6 +121,9 @@ def tile_dqn_pa_kernel(tc, x, h1, W2, b2, W3, b3, out):
                     dst = units[gp][:].bitcast(F32).rearrange("p (g b u) -> p g b u", g=2, u=2)
                     dst = dst[:, :, ii * P:(ii + 1) * P, :]
                     nc.scalar.copy(out=dst, in_=bank[:].rearrange("p g u b -> p g b u"))
+
+        def h1_quantise(bh):
+            units = h1g[bh]
             for c in range(4):
                 nc.vector.quantize_mx(
                     out=h1codes[:, c, 512 * bh:512 * bh + 512].bitcast(FP8X4),
@@ -169,14 +178,14 @@ def tile_dqn_pa_kernel(tc, x, h1, W2, b2, W3, b3, out):
         def epilogue(u, groups):
             g, i0, nb = UNITS[u]
             n = P * nb
-            a = big.tile([P, 4, n], F32, name="a%d" % u, tag="big", align_bytes=64)
+            a = big.tile([P, P, 4, 4], F32, name="a%d" % u, tag="big", align_bytes=64)
             for t in range(4):
-                nc.scalar.activation(out=a[:, t, :], in_=groups[t], func=ACT.Identity,
-                                     bias=b2T[:, 4 * g + t:4 * g + t + 1], scale=1.0)
-            h2g = h2gp.tile([P, n, 4], BF16, name="h2g%d" % u, tag="h2g", align_bytes=64)
-            av = a[:].rearrange("p t b -> p b t")
-            nc.vector.scalar_tensor_tensor(out=h2g[:], in0=av, scalar=SLOPE, in1=av,
-                                           op0=ALU.mult, op1=ALU.max)
+                nc.scalar.activation(out=a[:, :, t, :], in_=groups[t].rearrange("p (c i) -> p c i", i=4),
+                                     func=ACT.Identity, bias=b2T[:, 4 * g + t:4 * g + t + 1], scale=1.0)
+            h2g = h2gp.tile([P, 4, P, 4], BF16, name="h2g%d" % u, tag="h2g", align_bytes=64)
+            av = a[:].rearrange("p c t i -> p (c t) i")
+            nc.vector.scalar_tensor_tensor(out=h2g[:].rearrange("p i c t -> p (c t) i"), in0=av,
+                                           scalar=SLOPE, in1=av, op0=ALU.mult, op1=ALU.max)
             return h2g
 
         def h2_quantise(u, h2g):
@@ -185,7 +194,7 @@ def tile_dqn_pa_kernel(tc, x, h1, W2, b2, W3, b3, out):
             nc.vector.quantize_mx(
                 out=h2codes[:, g, P * i0:P * i0 + n].bitcast(FP8X4),
                 scales=h2sc[:, g, P * i0:P * i0 + n],
-                in_=h2g[:].rearrange("p b t -> p (b t)"),
+                in_=h2g[:].rearrange("p i c t -> p (i c t)"),
             )
 
         def head(j):
@@ -216,8 +225,10 @@ def tile_dqn_pa_kernel(tc, x, h1, W2, b2, W3, b3, out):
             nc.vector.reciprocal(out=r[:], in_=s[:])
             for ii in range(HEAD):
                 nc.scalar.activation(out=e[:, ii, :], in_=e[:, ii, :], func=ACT.Copy, scale=r[:, ii:ii + 1])
-            rows = P * HEAD
-            nc.sync.dma_start(out=out[rows * j:rows * (j + 1), :].rearrange("(i p) a -> p i a", p=P), in_=e[:])
+            i0 = HEAD * j
+            r0 = i0 // 4 * 4 * P
+            rows = out[r0:r0 + 4 * P, :].rearrange("(p i) a -> p i a", i=4)
+            nc.sync.dma_start(out=rows[:, i0 % 4:i0 % 4 + HEAD, :], in_=e[:])
 
         nbm = const.tile([P, 8, A], F32, name="nbm")
         for (i0, n, t) in xparts:
@@ -227,6 +238,7 @@ def tile_dqn_pa_kernel(tc, x, h1, W2, b2, W3, b3, out):
                                         axis=AX.X, op=ALU.add)
 
         h1_half(0)
+        h1_quantise(0)
         h1_half(1)
 
         b2rows32 = const.tile([P, P], F32, name="b2rows32")
@@ -236,16 +248,18 @@ def tile_dqn_pa_kernel(tc, x, h1, W2, b2, W3, b3, out):
         b2T = const.tile([P, 16], F32, name="b2T")
         nc.vector.tensor_copy(out=b2T[:], in_=b2ps[:, 0:16])
 
+        for k in range(4):
+            w2_regroup(k)
+        for k in range(4):
+            w2_quantise(k)
+        h1_quantise(1)
+
         b3ps = psum.tile([P, 512], F32, name="b3ps", tag="bank")
         nc.tensor.matmul(out=b3ps[:, 0:A], lhsT=tiny[:], rhs=b3row[:], start=True, stop=True)
         nc.vector.scalar_tensor_tensor(out=nbm[:], in0=nbm[:], scalar=0.0,
                                        in1=b3ps[:, 0:A].unsqueeze(1).to_broadcast([P, 8, A]),
                                        op0=ALU.is_equal, op1=ALU.subtract)
 
-        for k in range(4):
-            w2_regroup(k)
-        for k in range(4):
-            w2_quantise(k)
         nxt = 4
         waiting = []
         heads = 0
@@ -264,7 +278,8 @@ def tile_dqn_pa_kernel(tc, x, h1, W2, b2, W3, b3, out):
                 w2_quantise(k)
             if u == 5:
                 w3g = const.tile([P, 4, A, 4], BF16, name="w3g", align_bytes=64)
-                nc.scalar.copy(out=w3g[:], in_=w3raw[:].rearrange("p g t a -> p g a t"))
+                nc.scalar.copy(out=w3g[:].rearrange("p g (c i) t -> p g c t i", i=8),
+                               in_=w3raw[:].rearrange("p g t (c i) -> p g c t i", i=8))
                 nc.vector.quantize_mx(out=w3codes[:].bitcast(FP8X4), scales=w3sc[:],
                                       in_=w3g[:].rearrange("p g a t -> p (g a t)"))
             if done:

@@ -21,7 +21,7 @@ FLOPS = 2 * B * H1 * H2 + 2 * B * H2 * A
 WVS = (256, 192, 192, 128)
 RUN = 8
 LAG = 1
-UNITS = [(g, i0, 4) for g in range(4) for i0 in (0, 4)]
+UNITS = [(g, h, 0, P) for g in range(4) for h in range(2)][:-1] + [(3, 1, 0, 64), (3, 1, 64, 64)]
 HEAD = 2
 
 
@@ -48,6 +48,7 @@ def tile_dqn_pa_kernel(tc, x, h1, W2, b2, W3, b3, out):
             nc.scalar.dma_start(out=b2rows[4 * g:4 * g + 4, :].rearrange("b (q i) -> b q i", i=RUN), in_=b2v[g])
         b3row = const.tile([P, A], BF16, name="b3row")
         nc.vector.memset(b3row[:], 0.0)
+        nc.scalar.dma_start(out=b3row[0:1, :], in_=b3.rearrange("(o a) -> o a", o=1))
         tiny = const.tile([P, P], BF16, name="tiny")
         nc.vector.memset(tiny[:], 1.0 / BIG)
 
@@ -86,7 +87,6 @@ def tile_dqn_pa_kernel(tc, x, h1, W2, b2, W3, b3, out):
         load_x(6, 2)
         for i in range(5, 8):
             load_h1(i)
-        nc.sync.dma_start(out=b3row[0:1, :], in_=b3.rearrange("(o a) -> o a", o=1))
         w2raw = []
         for k in range(16):
             g, c = k // 4, k % 4
@@ -104,6 +104,18 @@ def tile_dqn_pa_kernel(tc, x, h1, W2, b2, W3, b3, out):
 
         h1g = {}
 
+        b2rows32 = const.tile([P, P], F32, name="b2rows32")
+        biases = const.tile([P, 2 * P], F32, name="biases")
+        b2T = biases[:, 0:16]
+        b3all = biases[:, P:2 * P]
+
+        def spread_biases():
+            nc.vector.tensor_copy(out=b2rows32[:], in_=b2rows[:])
+            bps = psum.tile([P, 512], F32, name="bps", tag="bank")
+            nc.tensor.transpose(bps[:, 0:P], b2rows32[:], ident[:])
+            nc.tensor.matmul(out=bps[:, P:2 * P], lhsT=tiny[:], rhs=b3row[:], start=True, stop=True)
+            nc.vector.tensor_copy(out=biases[:], in_=bps[:, 0:2 * P])
+
         def h1_half(bh):
             units = [
                 big.tile([P, 2 * 512 * 4], BF16, name="h1g%d_%d" % (bh, gp), tag="big", align_bytes=64)
@@ -112,6 +124,8 @@ def tile_dqn_pa_kernel(tc, x, h1, W2, b2, W3, b3, out):
             h1g[bh] = units
             for ii in range(4):
                 words = h1raw[4 * bh + ii][:].bitcast(F32)
+                if bh == 0 and ii == 2:
+                    spread_biases()
                 for gp in range(2):
                     bank = psum.tile([P, 2, 2, P], F32, name="trb%d_%d_%d" % (bh, ii, gp), tag="bank")
                     for gg in range(2):
@@ -153,8 +167,8 @@ def tile_dqn_pa_kernel(tc, x, h1, W2, b2, W3, b3, out):
             )
 
         def mm1(u, c_outer):
-            g, i0, nb = UNITS[u]
-            n = P * nb
+            g, h, c0, nc4 = UNITS[u]
+            b0, n = 512 * h + 4 * c0, 4 * nc4
             per = 512 // n
             banks = [psum.tile([P, per, n], F32, name="mm%d_%d" % (u, j), tag="bank") for j in range(4 // per)]
             groups = [banks[t // per][:, t % per, :] for t in range(4)]
@@ -168,34 +182,38 @@ def tile_dqn_pa_kernel(tc, x, h1, W2, b2, W3, b3, out):
                     out=groups[t],
                     lhsT=w2codes[:, c, m * P:(m + 1) * P].bitcast(FP8X4),
                     lhsT_scale=w2sc[:, c, m * P:(m + 1) * P],
-                    rhs=h1codes[:, c, P * i0:P * i0 + n].bitcast(FP8X4),
-                    rhs_scale=h1sc[:, c, P * i0:P * i0 + n],
+                    rhs=h1codes[:, c, b0:b0 + n].bitcast(FP8X4),
+                    rhs_scale=h1sc[:, c, b0:b0 + n],
                     start=(c == 0),
                     stop=(c == 3),
                 )
             return groups
 
         def epilogue(u, groups):
-            g, i0, nb = UNITS[u]
-            n = P * nb
-            a = big.tile([P, P, 4, 4], F32, name="a%d" % u, tag="big", align_bytes=64)
+            g, h, c0, nc4 = UNITS[u]
+            a = big.tile([P, nc4, 4, 4], F32, name="a%d" % u, tag="big", align_bytes=64)
             for t in range(4):
                 nc.scalar.activation(out=a[:, :, t, :], in_=groups[t].rearrange("p (c i) -> p c i", i=4),
                                      func=ACT.Identity, bias=b2T[:, 4 * g + t:4 * g + t + 1], scale=1.0)
-            h2g = h2gp.tile([P, 4, P, 4], BF16, name="h2g%d" % u, tag="h2g", align_bytes=64)
+            h2g = h2gp.tile([P, 4, nc4, 4], BF16, name="h2g%d" % u, tag="h2g", align_bytes=64)
             av = a[:].rearrange("p c t i -> p (c t) i")
             nc.vector.scalar_tensor_tensor(out=h2g[:].rearrange("p i c t -> p (c t) i"), in0=av,
                                            scalar=SLOPE, in1=av, op0=ALU.mult, op1=ALU.max)
             return h2g
 
         def h2_quantise(u, h2g):
-            g, i0, nb = UNITS[u]
-            n = P * nb
-            nc.vector.quantize_mx(
-                out=h2codes[:, g, P * i0:P * i0 + n].bitcast(FP8X4),
-                scales=h2sc[:, g, P * i0:P * i0 + n],
-                in_=h2g[:].rearrange("p i c t -> p (i c t)"),
-            )
+            g, h, c0, nc4 = UNITS[u]
+            if nc4 == P:
+                pieces = [(0, 4)]
+            else:
+                pieces = [(i, 1) for i in range(4)]
+            for (i, m) in pieces:
+                b0 = 512 * h + P * i + c0
+                nc.vector.quantize_mx(
+                    out=h2codes[:, g, b0:b0 + m * nc4].bitcast(FP8X4),
+                    scales=h2sc[:, g, b0:b0 + m * nc4],
+                    in_=h2g[:, i:i + m].rearrange("p i c t -> p (i c t)"),
+                )
 
         def head(j):
             lg = psum.tile([P, HEAD, A], F32, name="lg%d" % j, tag="bank")
@@ -239,14 +257,11 @@ def tile_dqn_pa_kernel(tc, x, h1, W2, b2, W3, b3, out):
 
         h1_half(0)
         h1_quantise(0)
+        for (i0, n, t) in xparts:
+            nc.vector.scalar_tensor_tensor(out=nbm[:, i0:i0 + n, :], in0=nbm[:, i0:i0 + n, :], scalar=0.0,
+                                           in1=b3all.unsqueeze(1).to_broadcast([P, n, A]),
+                                           op0=ALU.is_equal, op1=ALU.subtract)
         h1_half(1)
-
-        b2rows32 = const.tile([P, P], F32, name="b2rows32")
-        nc.vector.tensor_copy(out=b2rows32[:], in_=b2rows[:])
-        b2ps = psum.tile([P, 512], F32, name="b2ps", tag="bank")
-        nc.tensor.transpose(b2ps[:, 0:P], b2rows32[:], ident[:])
-        b2T = const.tile([P, 16], F32, name="b2T")
-        nc.vector.tensor_copy(out=b2T[:], in_=b2ps[:, 0:16])
 
         for k in range(4):
             w2_regroup(k)
@@ -254,29 +269,21 @@ def tile_dqn_pa_kernel(tc, x, h1, W2, b2, W3, b3, out):
             w2_quantise(k)
         h1_quantise(1)
 
-        b3ps = psum.tile([P, 512], F32, name="b3ps", tag="bank")
-        nc.tensor.matmul(out=b3ps[:, 0:A], lhsT=tiny[:], rhs=b3row[:], start=True, stop=True)
-        nc.vector.scalar_tensor_tensor(out=nbm[:], in0=nbm[:], scalar=0.0,
-                                       in1=b3ps[:, 0:A].unsqueeze(1).to_broadcast([P, 8, A]),
-                                       op0=ALU.is_equal, op1=ALU.subtract)
-
         nxt = 4
         waiting = []
-        heads = 0
-        covered = 0
         for u in range(len(UNITS)):
             waiting.append((u, mm1(u, u == 0)))
             ks = range(nxt, min(nxt + 2, 16))
             nxt += 2
-            for k in ks:
-                w2_regroup(k)
             done = None
             if len(waiting) > LAG:
                 (v, groups) = waiting.pop(0)
                 done = (v, epilogue(v, groups))
             for k in ks:
+                w2_regroup(k)
+            for k in ks:
                 w2_quantise(k)
-            if u == 5:
+            if u == 6:
                 w3g = const.tile([P, 4, A, 4], BF16, name="w3g", align_bytes=64)
                 nc.scalar.copy(out=w3g[:].rearrange("p g (c i) t -> p g c t i", i=8),
                                in_=w3raw[:].rearrange("p g t (c i) -> p g c t i", i=8))
@@ -284,13 +291,7 @@ def tile_dqn_pa_kernel(tc, x, h1, W2, b2, W3, b3, out):
                                       in_=w3g[:].rearrange("p g a t -> p (g a t)"))
             if done:
                 h2_quantise(done[0], done[1])
-                if UNITS[done[0]][0] == 3:
-                    covered += UNITS[done[0]][2]
-            if covered >= HEAD * (heads + 2):
-                head(heads)
-                heads += 1
         for (v, groups) in waiting:
             h2_quantise(v, epilogue(v, groups))
-        while heads * HEAD < 8:
-            head(heads)
-            heads += 1
+        for j in range(8 // HEAD):
+            head(j)

from contextlib import ExitStack

import concourse.mybir as mybir
from concourse.masks import make_identity

F32 = mybir.dt.float32
BF16 = mybir.dt.bfloat16
U32 = mybir.dt.uint32
U8 = mybir.dt.uint8
FP8X4 = mybir.dt.float8_e4m3fn_x4
ALU = mybir.AluOpType
ACT = mybir.ActivationFunctionType
AX = mybir.AxisListType

P = 128
B, A, G, H1, H2 = 1024, 128, 5, 2048, 2048
SLOPE = 0.4
BIG = 2.0 ** 100
FLOPS = 2 * B * H1 * H2 + 2 * B * H2 * A

WVS = (256, 192, 192, 128)
RUN = 8
LAG = 1
UNITS = [(g, h, 0, P) for g in range(4) for h in range(2)][:-1] + [(3, 1, 0, 64), (3, 1, 64, 64)]
HEAD = 2


def tile_dqn_pa_kernel(tc, x, h1, W2, b2, W3, b3, out):
    nc = tc.nc
    with ExitStack() as ctx:
        const = ctx.enter_context(tc.tile_pool(name="const", bufs=1))
        raw = ctx.enter_context(tc.tile_pool(name="raw", bufs=12))
        big = ctx.enter_context(tc.tile_pool(name="big", bufs=5))
        w2gp = ctx.enter_context(tc.tile_pool(name="w2gp", bufs=4))
        h2gp = ctx.enter_context(tc.tile_pool(name="h2gp", bufs=2))
        sm = ctx.enter_context(tc.tile_pool(name="sm", bufs=4))
        psum = ctx.enter_context(tc.psum_pool(name="psum", bufs=8))

        ident = const.tile([P, P], F32, name="ident")
        make_identity(nc, ident[:])
        warm = const.tile([P, 2], F32, name="warm")
        nc.vector.memset(warm[:], 0.0)
        nc.scalar.activation(out=warm[:, 1:2], in_=warm[:, 0:1], func=ACT.Exp)
        b2rows = const.tile([P, P], BF16, name="b2rows")
        nc.vector.memset(b2rows[:], 0.0)
        b2v = b2.rearrange("(g q b i) -> g b q i", g=4, b=4, i=RUN)
        for g in range(4):
            nc.scalar.dma_start(out=b2rows[4 * g:4 * g + 4, :].rearrange("b (q i) -> b q i", i=RUN), in_=b2v[g])
        b3row = const.tile([P, A], BF16, name="b3row")
        nc.vector.memset(b3row[:], 0.0)
        nc.scalar.dma_start(out=b3row[0:1, :], in_=b3.rearrange("(o a) -> o a", o=1))
        tiny = const.tile([P, P], BF16, name="tiny")
        nc.vector.memset(tiny[:], 1.0 / BIG)

        h1codes = const.tile([P, 4, B], U32, name="h1codes", align_bytes=64)
        h1sc = const.tile([P, 4, B], U8, name="h1sc", align_bytes=64)
        w2codes = const.tile([P, 4, H2], U32, name="w2codes", align_bytes=64)
        w2sc = const.tile([P, 4, H2], U8, name="w2sc", align_bytes=64)
        h2codes = const.tile([P, 4, B], U32, name="h2codes", align_bytes=64)
        h2sc = const.tile([P, 4, B], U8, name="h2sc", align_bytes=64)
        w3codes = const.tile([P, 4 * A], U32, name="w3codes", align_bytes=64)
        w3sc = const.tile([P, 4 * A], U8, name="w3sc", align_bytes=64)

        xparts = []
        h1raw = []

        def load_x(i0, n):
            r0 = i0 // 4 * 4 * P
            t = raw.tile([P, n, A * G], BF16, name="xraw%d" % i0, tag="raw")
            rows = x[r0:r0 + 4 * P, :].rearrange("(p i) c -> p i c", i=4)
            nc.sync.dma_start(out=t[:], in_=rows[:, i0 % 4:i0 % 4 + n, :])
            xparts.append((i0, n, t))

        def load_h1(i):
            t = raw.tile([P, H1], BF16, name="h1raw%d" % i, tag="raw")
            nc.sync.dma_start(out=t[:], in_=h1[i * P:(i + 1) * P, :])
            h1raw.append(t)

        load_h1(0)
        load_x(0, 2)
        load_h1(1)
        load_x(2, 2)
        load_h1(2)
        load_x(4, 2)
        load_h1(3)
        load_h1(4)
        load_x(6, 2)
        for i in range(5, 8):
            load_h1(i)
        w2raw = []
        for k in range(16):
            g, c = k // 4, k % 4
            t = raw.tile([P, 4, 512], BF16, name="w2raw%d" % k, tag="raw")
            nc.sync.dma_start(
                out=t[:],
                in_=W2[512 * c:512 * c + 512, 512 * g:512 * g + 512].rearrange("(p t) w -> p t w", t=4),
            )
            w2raw.append(t)
        w3raw = raw.tile([P, 4, 4, A], BF16, name="w3raw", tag="raw")
        w3v = W3.rearrange("(g q b i) a -> g i q b a", g=4, b=4, i=RUN)
        for g in range(4):
            for i in range(RUN):
                nc.sync.dma_start(out=w3raw[i:P:RUN, g, :, :], in_=w3v[g, i])

        h1g = {}

        b2rows32 = const.tile([P, P], F32, name="b2rows32")
        biases = const.tile([P, 2 * P], F32, name="biases")
        b2T = biases[:, 0:16]
        b3all = biases[:, P:2 * P]

        def spread_biases():
            nc.vector.tensor_copy(out=b2rows32[:], in_=b2rows[:])
            bps = psum.tile([P, 512], F32, name="bps", tag="bank")
            nc.tensor.transpose(bps[:, 0:P], b2rows32[:], ident[:])
            nc.tensor.matmul(out=bps[:, P:2 * P], lhsT=tiny[:], rhs=b3row[:], start=True, stop=True)
            nc.vector.tensor_copy(out=biases[:], in_=bps[:, 0:2 * P])

        def h1_half(bh):
            units = [
                big.tile([P, 2 * 512 * 4], BF16, name="h1g%d_%d" % (bh, gp), tag="big", align_bytes=64)
                for gp in range(2)
            ]
            h1g[bh] = units
            for ii in range(4):
                words = h1raw[4 * bh + ii][:].bitcast(F32)
                if bh == 0 and ii == 2:
                    spread_biases()
                for gp in range(2):
                    bank = psum.tile([P, 2, 2, P], F32, name="trb%d_%d_%d" % (bh, ii, gp), tag="bank")
                    for gg in range(2):
                        for u in range(2):
                            w0 = 256 * (2 * gp + gg)
                            nc.tensor.transpose(bank[:, gg, u, :], words[:, w0 + u:w0 + 256:2], ident[:])
                    dst = units[gp][:].bitcast(F32).rearrange("p (g b u) -> p g b u", g=2, u=2)
                    dst = dst[:, :, ii * P:(ii + 1) * P, :]
                    nc.scalar.copy(out=dst, in_=bank[:].rearrange("p g u b -> p g b u"))

        def h1_quantise(bh):
            units = h1g[bh]
            for c in range(4):
                nc.vector.quantize_mx(
                    out=h1codes[:, c, 512 * bh:512 * bh + 512].bitcast(FP8X4),
                    scales=h1sc[:, c, 512 * bh:512 * bh + 512],
                    in_=units[c // 2][:, 2048 * (c % 2):2048 * (c % 2) + 2048],
                )

        w2grp = {}

        def w2_regroup(k):
            qv = WVS[k // 4] // (4 * RUN)
            src = w2raw[k]
            grp = w2gp.tile([P, 512, 4], BF16, name="w2g%d" % k, tag="w2g", align_bytes=64)
            dst = grp[:].rearrange("p (b q i) t -> p q b t i", b=4, i=RUN)
            src = src[:].rearrange("p t (q b i) -> p q b t i", b=4, i=RUN)
            nc.vector.tensor_copy(out=dst[:, 0:qv], in_=src[:, 0:qv])
            nc.scalar.copy(out=dst[:, qv:], in_=src[:, qv:])
            w2grp[k] = grp

        def w2_quantise(k):
            g, c = k // 4, k % 4
            grp = w2grp[k]
            nc.vector.quantize_mx(
                out=w2codes[:, c, 512 * g:512 * g + 512].bitcast(FP8X4),
                scales=w2sc[:, c, 512 * g:512 * g + 512],
                in_=grp[:].rearrange("p w t -> p (w t)"),
            )

        def mm1(u, c_outer):
            g, h, c0, nc4 = UNITS[u]
            b0, n = 512 * h + 4 * c0, 4 * nc4
            per = 512 // n
            banks = [psum.tile([P, per, n], F32, name="mm%d_%d" % (u, j), tag="bank") for j in range(4 // per)]
            groups = [banks[t // per][:, t % per, :] for t in range(4)]
            if c_outer:
                order = [(c, t) for c in range(4) for t in range(4)]
            else:
                order = [(c, t) for t in range(4) for c in range(4)]
            for (c, t) in order:
                m = 4 * g + t
                nc.tensor.matmul_mx(
                    out=groups[t],
                    lhsT=w2codes[:, c, m * P:(m + 1) * P].bitcast(FP8X4),
                    lhsT_scale=w2sc[:, c, m * P:(m + 1) * P],
                    rhs=h1codes[:, c, b0:b0 + n].bitcast(FP8X4),
                    rhs_scale=h1sc[:, c, b0:b0 + n],
                    start=(c == 0),
                    stop=(c == 3),
                )
            return groups

        def epilogue(u, groups):
            g, h, c0, nc4 = UNITS[u]
            a = big.tile([P, nc4, 4, 4], F32, name="a%d" % u, tag="big", align_bytes=64)
            for t in range(4):
                nc.scalar.activation(out=a[:, :, t, :], in_=groups[t].rearrange("p (c i) -> p c i", i=4),
                                     func=ACT.Identity, bias=b2T[:, 4 * g + t:4 * g + t + 1], scale=1.0)
            h2g = h2gp.tile([P, 4, nc4, 4], BF16, name="h2g%d" % u, tag="h2g", align_bytes=64)
            av = a[:].rearrange("p c t i -> p (c t) i")
            nc.vector.scalar_tensor_tensor(out=h2g[:].rearrange("p i c t -> p (c t) i"), in0=av,
                                           scalar=SLOPE, in1=av, op0=ALU.mult, op1=ALU.max)
            return h2g

        def h2_quantise(u, h2g):
            g, h, c0, nc4 = UNITS[u]
            if nc4 == P:
                pieces = [(0, 4)]
            else:
                pieces = [(i, 1) for i in range(4)]
            for (i, m) in pieces:
                b0 = 512 * h + P * i + c0
                nc.vector.quantize_mx(
                    out=h2codes[:, g, b0:b0 + m * nc4].bitcast(FP8X4),
                    scales=h2sc[:, g, b0:b0 + m * nc4],
                    in_=h2g[:, i:i + m].rearrange("p i c t -> p (i c t)"),
                )

        def head(j):
            lg = psum.tile([P, HEAD, A], F32, name="lg%d" % j, tag="bank")
            for ii in range(HEAD):
                i = HEAD * j + ii
                for g in range(4):
                    nc.tensor.matmul_mx(
                        out=lg[:, ii, :],
                        lhsT=h2codes[:, g, i * P:(i + 1) * P].bitcast(FP8X4),
                        lhsT_scale=h2sc[:, g, i * P:(i + 1) * P],
                        rhs=w3codes[:, g * A:(g + 1) * A].bitcast(FP8X4),
                        rhs_scale=w3sc[:, g * A:(g + 1) * A],
                        start=(g == 0),
                        stop=(g == 3),
                    )
            nlp = sm.tile([P, HEAD, A], F32, name="nlp%d" % j, tag="nlp")
            nc.vector.scalar_tensor_tensor(out=nlp[:], in0=nbm[:, HEAD * j:HEAD * (j + 1), :], scalar=BIG,
                                           in1=lg[:], op0=ALU.mult, op1=ALU.subtract)
            nmx = sm.tile([P, HEAD], F32, name="nmx%d" % j, tag="nmx")
            nc.vector.tensor_reduce(out=nmx[:], in_=nlp[:], axis=AX.X, op=ALU.min)
            e = sm.tile([P, HEAD, A], F32, name="e%d" % j, tag="e")
            s = sm.tile([P, HEAD], F32, name="s%d" % j, tag="s")
            for ii in range(HEAD):
                nc.scalar.activation(out=e[:, ii, :], in_=nlp[:, ii, :], func=ACT.Exp,
                                     bias=nmx[:, ii:ii + 1], scale=-1.0, accum_out=s[:, ii:ii + 1])
            r = sm.tile([P, HEAD], F32, name="r%d" % j, tag="r")
            nc.vector.reciprocal(out=r[:], in_=s[:])
            for ii in range(HEAD):
                nc.scalar.activation(out=e[:, ii, :], in_=e[:, ii, :], func=ACT.Copy, scale=r[:, ii:ii + 1])
            i0 = HEAD * j
            r0 = i0 // 4 * 4 * P
            rows = out[r0:r0 + 4 * P, :].rearrange("(p i) a -> p i a", i=4)
            nc.sync.dma_start(out=rows[:, i0 % 4:i0 % 4 + HEAD, :], in_=e[:])

        nbm = const.tile([P, 8, A], F32, name="nbm")
        for (i0, n, t) in xparts:
            for i in range(n):
                nc.vector.tensor_reduce(out=nbm[:, i0 + i, :],
                                        in_=t[:, i, :].rearrange("p (a j) -> p a j", j=G),
                                        axis=AX.X, op=ALU.add)

        h1_half(0)
        h1_quantise(0)
        for (i0, n, t) in xparts:
            nc.vector.scalar_tensor_tensor(out=nbm[:, i0:i0 + n, :], in0=nbm[:, i0:i0 + n, :], scalar=0.0,
                                           in1=b3all.unsqueeze(1).to_broadcast([P, n, A]),
                                           op0=ALU.is_equal, op1=ALU.subtract)
        h1_half(1)

        for k in range(4):
            w2_regroup(k)
        for k in range(4):
            w2_quantise(k)
        h1_quantise(1)

        nxt = 4
        waiting = []
        for u in range(len(UNITS)):
            waiting.append((u, mm1(u, u == 0)))
            ks = range(nxt, min(nxt + 2, 16))
            nxt += 2
            done = None
            if len(waiting) > LAG:
                (v, groups) = waiting.pop(0)
                done = (v, epilogue(v, groups))
            for k in ks:
                w2_regroup(k)
            for k in ks:
                w2_quantise(k)
            if u == 6:
                w3g = const.tile([P, 4, A, 4], BF16, name="w3g", align_bytes=64)
                nc.scalar.copy(out=w3g[:].rearrange("p g (c i) t -> p g c t i", i=8),
                               in_=w3raw[:].rearrange("p g t (c i) -> p g c t i", i=8))
                nc.vector.quantize_mx(out=w3codes[:].bitcast(FP8X4), scales=w3sc[:],
                                      in_=w3g[:].rearrange("p g a t -> p (g a t)"))
            if done:
                h2_quantise(done[0], done[1])
        for (v, groups) in waiting:
            h2_quantise(v, epilogue(v, groups))
        for j in range(8 // HEAD):
            head(j)
